import numpy as np
import ml_dtypes


def mxq(x, axis, fmt="e4m3"):
    dtype, down = {"e4m3": (ml_dtypes.float8_e4m3fn, 7), "e5m2": (ml_dtypes.float8_e5m2, 14)}[fmt]
    v = np.moveaxis(np.asarray(x, np.float32).astype(ml_dtypes.bfloat16).astype(np.float64), axis, -1)
    blocks = v.reshape(v.shape[:-1] + (-1, 32))
    amax = np.abs(blocks).max(-1, keepdims=True)
    byte = np.maximum(np.where(amax > 0, np.frexp(amax)[1] - 1 + 127, 0) - down, 1)
    scale = np.exp2(byte - 127.0)
    codes = (blocks / scale).astype(np.float32).astype(dtype).astype(np.float64)
    return np.moveaxis((codes * scale).reshape(v.shape), -1, axis)


WIDE = False


def mx_kscale(k):
    if not WIDE:
        return np.ones(k)
    levels = np.array([10, -10, 5, -5, 0])
    a = np.random.permutation(np.resize(levels, k // 512 * 4)).reshape(k // 512, 4)
    idx = np.arange(k)
    return np.exp2(a[idx // 512, idx % 128 // 32])


BF16 = ml_dtypes.bfloat16


def bf(x):
    return np.asarray(x, np.float32).astype(BF16)


def f64(x):
    return np.asarray(x).astype(np.float64)


B, T, N, DH, D = 1, 128, 4, 128, 512
KC = N * DH


def setup_inputs():
    r = np.random.standard_normal
    s = mx_kscale(D)
    t = mx_kscale(KC).reshape(N, DH)
    return {"normalized_resid_pre": bf(r((B, T, D)) * s),
            "W_C": bf(r((N, D, DH)) / np.sqrt(D) / s[None, :, None] * t[:, None, :]),
            "b_C": bf(0.1 * r((N, DH)) * t),
            "W_K": bf(1.3 / np.sqrt(KC) * r((N, DH, DH, DH)) / t[:, None, None, :])}


def reference(normalized_resid_pre, W_C, b_C, W_K):
    x = f64(normalized_resid_pre)
    wc = f64(W_C).transpose(1, 0, 2).reshape(D, KC)
    c = (mxq(x, 2, "e4m3") @ mxq(wc, 0, "e4m3")) + f64(b_C).reshape(KC)
    wk = f64(W_K).transpose(0, 3, 1, 2).reshape(KC, DH * DH)
    step1 = mxq(c, 2, "e4m3") @ mxq(wk, 0, "e4m3")
    return step1.reshape(B, T, DH, DH)

@@ -1,0 +1,219 @@
+from contextlib import ExitStack
+
+import concourse.mybir as mybir
+from concourse.masks import make_identity
+
+F32 = mybir.dt.float32
+BF16 = mybir.dt.bfloat16
+U32 = mybir.dt.uint32
+U8 = mybir.dt.uint8
+FP8X4 = mybir.dt.float8_e4m3fn_x4
+ADD = mybir.AluOpType.add
+
+P = 128
+PACK = 4
+TOKENS = 128
+D_MODEL = 512
+HEADS = 4
+D_HEAD = 128
+JOINT = HEADS * D_HEAD
+OUT_COLS = D_HEAD * D_HEAD
+HALF = 64
+
+ROWS = 16
+CHUNK = P * ROWS
+CHUNKS = OUT_COLS // CHUNK
+STEPS = 2 * CHUNKS
+WINDOWS = ROWS // 2
+STEP_COLS = WINDOWS * P
+BANK_WINDOWS = 2
+STEP_BANKS = WINDOWS // BANK_WINDOWS
+GROUP_COLS = BANK_WINDOWS * P
+
+RAW_BUFS = 8
+LAG = 3
+
+FLOPS = 2 * TOKENS * D_MODEL * JOINT + 2 * TOKENS * JOINT * OUT_COLS
+
+
+def tile_trittentioncube_pa_kernel(tc, normalized_resid_pre, W_C, b_C, W_K, out):
+    nc = tc.nc
+    wk_rows = W_K.rearrange("n i j k -> n (i j) k")
+    out_cols = out.rearrange("o t i j -> (o t) (i j)")
+
+    with ExitStack() as ctx:
+        keep = ctx.enter_context(tc.tile_pool(name="keep", bufs=1))
+        raw_pool = ctx.enter_context(tc.tile_pool(name="raw", bufs=RAW_BUFS))
+        grouped_pool = ctx.enter_context(tc.tile_pool(name="grouped", bufs=3))
+        quantised_pool = ctx.enter_context(tc.tile_pool(name="quantised", bufs=6))
+        result_pool = ctx.enter_context(tc.tile_pool(name="result", bufs=3))
+        xt_pool = ctx.enter_context(tc.psum_pool(name="xt", bufs=4))
+        acc_pool = ctx.enter_context(tc.psum_pool(name="acc", bufs=4))
+
+        def load_wk(step):
+            chunk, pair = divmod(step, 2)
+            raw = raw_pool.tile([P, 2 * ROWS * D_HEAD], BF16)
+            rows = wk_rows[2 * pair : 2 * pair + 2, chunk * CHUNK : (chunk + 1) * CHUNK, :]
+            nc.sync.dma_start(
+                out=raw[:].rearrange("p (a x) -> p a x", a=2),
+                in_=rows.rearrange("a (p r) k -> p a (r k)", p=P),
+            )
+            return raw
+
+        x_sb = keep.tile([P, D_MODEL], BF16)
+        nc.sync.dma_start(out=x_sb[:], in_=normalized_resid_pre.rearrange("o t d -> (o t) d"))
+        wc_raw = keep.tile([P, HEADS, PACK, D_HEAD], BF16)
+        nc.sync.dma_start(out=wc_raw[:], in_=W_C.rearrange("n (p j) k -> p n j k", j=PACK))
+        bias_row = keep.tile([P, JOINT], BF16)
+        nc.vector.memset(bias_row[:], 0.0)
+        nc.scalar.dma_start(out=bias_row[0:1, :], in_=b_C.rearrange("(o n) k -> o (n k)", o=1))
+        raw_tiles = {}
+        for step in range(RAW_BUFS):
+            raw_tiles[step] = load_wk(step)
+
+        ident_f32 = keep.tile([P, P], F32)
+        make_identity(nc, ident_f32[:])
+        ident_bf16 = keep.tile([P, P], BF16)
+        make_identity(nc, ident_bf16[:])
+        ones = keep.tile([P, P], BF16)
+        nc.vector.memset(ones[:], 1.0)
+        c_grouped = keep.tile([P, 2, 2, TOKENS, PACK], BF16, align_bytes=64)
+        nc.vector.memset(c_grouped[:], 0.0)
+
+        bias_acc = acc_pool.tile([P, JOINT], F32, tag="acc")
+        nc.tensor.matmul(out=bias_acc[:], lhsT=ones[:], rhs=bias_row[:], start=True, stop=True)
+        bias_sb = keep.tile([P, JOINT], F32)
+        nc.scalar.copy(out=bias_sb[:], in_=bias_acc[:])
+
+        x_words = x_sb[:].bitcast(F32).rearrange("t (p j) -> t j p", j=2)
+        x_t = acc_pool.tile([P, 2, TOKENS], F32, tag="acc")
+        for j in range(2):
+            nc.tensor.transpose(x_t[:, j, :], x_words[:, j, :], ident_f32[:])
+        x_grouped = keep.tile([P, TOKENS * PACK], BF16, align_bytes=64)
+        nc.vector.tensor_copy(
+            out=x_grouped[:].bitcast(F32).rearrange("p (t j) -> p t j", j=2),
+            in_=x_t[:].rearrange("p j t -> p t j"),
+        )
+        x_codes = keep.tile([P, TOKENS], U32, align_bytes=64)
+        x_scales = keep.tile([P, TOKENS], U8, align_bytes=64)
+
+        wc_grouped = keep.tile([P, HEADS, D_HEAD, PACK], BF16, align_bytes=64)
+        nc.vector.tensor_copy(out=wc_grouped[:], in_=wc_raw[:].rearrange("p n j k -> p n k j"))
+        wc_codes = keep.tile([P, JOINT], U32, align_bytes=64)
+        wc_scales = keep.tile([P, JOINT], U8, align_bytes=64)
+        nc.vector.quantize_mx(
+            out=x_codes[:].bitcast(FP8X4), scales=x_scales[:], in_=x_grouped[:]
+        )
+        nc.vector.quantize_mx(
+            out=wc_codes[:].bitcast(FP8X4),
+            scales=wc_scales[:],
+            in_=wc_grouped[:].rearrange("p n k j -> p (n k j)"),
+        )
+
+        c_acc = acc_pool.tile([P, JOINT], F32, tag="acc")
+        nc.tensor.matmul_mx(
+            out=c_acc[:],
+            lhsT=x_codes[:].bitcast(FP8X4),
+            lhsT_scale=x_scales[:],
+            rhs=wc_codes[:].bitcast(FP8X4),
+            rhs_scale=wc_scales[:],
+            start=True,
+            stop=True,
+        )
+        c_sorted = keep.tile([P, HEADS, 2, 2, HALF], BF16)
+        for copy in range(2):
+            nc.vector.tensor_tensor(
+                out=c_sorted[:, :, :, copy, :],
+                in0=c_acc[:].rearrange("t (n w e) -> t n e w", n=HEADS, e=2),
+                in1=bias_sb[:].rearrange("t (n w e) -> t n e w", n=HEADS, e=2),
+                op=ADD,
+            )
+        c_t = acc_pool.tile([P, HEADS * 2, TOKENS], BF16, tag="acc")
+        for n in range(HEADS):
+            for e in range(2):
+                nc.tensor.transpose(
+                    c_t[:, 2 * n + e, :],
+                    c_sorted[:, n, e, :, :].rearrange("t c w -> t (c w)"),
+                    ident_bf16[:],
+                )
+        for half in range(2):
+            partitions = slice(half * HALF, (half + 1) * HALF)
+            nc.vector.tensor_copy(
+                out=c_grouped[partitions, half, :, :, :],
+                in_=c_t[partitions, :, :].rearrange("q (u x) t -> q u t x", u=2),
+            )
+        c_codes = keep.tile([P, 4 * TOKENS], U32, align_bytes=64)
+        c_scales = keep.tile([P, 4 * TOKENS], U8, align_bytes=64)
+        nc.vector.quantize_mx(
+            out=c_codes[:].bitcast(FP8X4),
+            scales=c_scales[:],
+            in_=c_grouped[:].rearrange("q h u t x -> q (h u t x)"),
+        )
+
+        def transpose_wk(raw):
+            words = raw[:].bitcast(F32).rearrange("p (a s w) -> p a s w", a=2, s=WINDOWS)
+            grouped = grouped_pool.tile([P, STEP_COLS * PACK], BF16, align_bytes=64)
+            grouped_words = grouped[:].bitcast(F32).rearrange("q (s p a) -> q s p a", p=P, a=2)
+            for bank in range(STEP_BANKS):
+                first = bank * BANK_WINDOWS
+                xt = xt_pool.tile([P, BANK_WINDOWS, 2, P], F32)
+                for s in range(BANK_WINDOWS):
+                    for a in range(2):
+                        nc.tensor.transpose(xt[:, s, a, :], words[:, a, first + s, :], ident_f32[:])
+                nc.scalar.copy(
+                    out=grouped_words[:, first : first + BANK_WINDOWS, :, :],
+                    in_=xt[:].rearrange("q s a p -> q s p a"),
+                )
+            return grouped
+
+        def quantise_wk(grouped):
+            codes = quantised_pool.tile([P, STEP_COLS], U32, align_bytes=64)
+            scales = quantised_pool.tile([P, STEP_COLS], U8, align_bytes=64)
+            nc.vector.quantize_mx(out=codes[:].bitcast(FP8X4), scales=scales[:], in_=grouped[:])
+            return codes, scales
+
+        def multiply(chunk, part, result):
+            sorted_result = result[:].rearrange(
+                "t (p b s h) -> t b p s h", b=STEP_BANKS, s=BANK_WINDOWS, h=2
+            )
+            for bank in (2 * part, 2 * part + 1):
+                cols = slice(bank * GROUP_COLS, (bank + 1) * GROUP_COLS)
+                acc = acc_pool.tile([P, 2, GROUP_COLS], F32, tag="acc")
+                for half in range(2):
+                    for pair in range(2):
+                        codes, scales = quantised[2 * chunk + pair]
+                        tokens = slice((2 * half + pair) * TOKENS, (2 * half + pair + 1) * TOKENS)
+                        nc.tensor.matmul_mx(
+                            out=acc[:, half, :],
+                            lhsT=c_codes[:, tokens].bitcast(FP8X4),
+                            lhsT_scale=c_scales[:, tokens],
+                            rhs=codes[:, cols].bitcast(FP8X4),
+                            rhs_scale=scales[:, cols],
+                            start=(pair == 0),
+                            stop=(pair == 1),
+                        )
+                nc.vector.tensor_copy(
+                    out=sorted_result[:, bank],
+                    in_=acc[:].rearrange("t h (s p) -> t p s h", s=BANK_WINDOWS),
+                )
+
+        grouped_tiles = {}
+        quantised = {}
+        results = {}
+        for step in range(STEPS + LAG):
+            if step < STEPS:
+                grouped_tiles[step] = transpose_wk(raw_tiles[step])
+                if step + RAW_BUFS < STEPS:
+                    raw_tiles[step + RAW_BUFS] = load_wk(step + RAW_BUFS)
+            if 1 <= step <= STEPS:
+                quantised[step - 1] = quantise_wk(grouped_tiles[step - 1])
+            if step >= LAG:
+                chunk, part = divmod(step - LAG, 2)
+                if part == 0:
+                    result = result_pool.tile([P, CHUNK], F32)
+                    results[chunk] = result
+                multiply(chunk, part, results[chunk])
+                if part == 1:
+                    nc.sync.dma_start(
+                        out=out_cols[:, chunk * CHUNK : (chunk + 1) * CHUNK], in_=results[chunk][:]
+                    )

@@ -42,6 +42,7 @@ def tile_trittentioncube_pa_kernel(tc, normalized_resid_pre, W_C, b_C, W_K, out)
     out_cols = out.rearrange("o t i j -> (o t) (i j)")
 
     with ExitStack() as ctx:
+        ctx.enter_context(tc.manual_schedule())
         keep = ctx.enter_context(tc.tile_pool(name="keep", bufs=1))
         raw_pool = ctx.enter_context(tc.tile_pool(name="raw", bufs=RAW_BUFS))
         grouped_pool = ctx.enter_context(tc.tile_pool(name="grouped", bufs=3))
@@ -49,6 +50,28 @@ def tile_trittentioncube_pa_kernel(tc, normalized_resid_pre, W_C, b_C, W_K, out)
         result_pool = ctx.enter_context(tc.tile_pool(name="result", bufs=3))
         xt_pool = ctx.enter_context(tc.psum_pool(name="xt", bufs=4))
         acc_pool = ctx.enter_context(tc.psum_pool(name="acc", bufs=4))
+
+        x_sb = keep.tile([P, D_MODEL], BF16)
+        wc_raw = keep.tile([P, HEADS, PACK, D_HEAD], BF16)
+        bias_row = keep.tile([P, JOINT], BF16)
+        bias_sb = keep.tile([P, JOINT], F32)
+        ident_f32 = keep.tile([P, P], F32)
+        ident_bf16 = keep.tile([P, P], BF16)
+        ones = keep.tile([P, P], BF16)
+        x_grouped = keep.tile([P, TOKENS * PACK], BF16, align_bytes=64)
+        x_codes = keep.tile([P, TOKENS], U32, align_bytes=64)
+        x_scales = keep.tile([P, TOKENS], U8, align_bytes=64)
+        wc_grouped = keep.tile([P, HEADS, D_HEAD, PACK], BF16, align_bytes=64)
+        wc_codes = keep.tile([P, JOINT], U32, align_bytes=64)
+        wc_scales = keep.tile([P, JOINT], U8, align_bytes=64)
+        c_sorted = keep.tile([P, HEADS, 2, 2, HALF], BF16)
+        c_grouped = keep.tile([P, 2, 2, TOKENS, PACK], BF16, align_bytes=64)
+        c_codes = keep.tile([P, 4 * TOKENS], U32, align_bytes=64)
+        c_scales = keep.tile([P, 4 * TOKENS], U8, align_bytes=64)
+        raw_tiles = {}
+        grouped_tiles = {}
+        quantised = {}
+        results = {}
 
         def load_wk(step):
             chunk, pair = divmod(step, 2)
@@ -58,100 +81,86 @@ def tile_trittentioncube_pa_kernel(tc, normalized_resid_pre, W_C, b_C, W_K, out)
                 out=raw[:].rearrange("p (a x) -> p a x", a=2),
                 in_=rows.rearrange("a (p r) k -> p a (r k)", p=P),
             )
-            return raw
+            raw_tiles[step] = raw
 
-        x_sb = keep.tile([P, D_MODEL], BF16)
-        nc.sync.dma_start(out=x_sb[:], in_=normalized_resid_pre.rearrange("o t d -> (o t) d"))
-        wc_raw = keep.tile([P, HEADS, PACK, D_HEAD], BF16)
-        nc.sync.dma_start(out=wc_raw[:], in_=W_C.rearrange("n (p j) k -> p n j k", j=PACK))
-        bias_row = keep.tile([P, JOINT], BF16)
-        nc.vector.memset(bias_row[:], 0.0)
-        nc.scalar.dma_start(out=bias_row[0:1, :], in_=b_C.rearrange("(o n) k -> o (n k)", o=1))
-        raw_tiles = {}
-        for step in range(RAW_BUFS):
-            raw_tiles[step] = load_wk(step)
+        def start_loads_and_constants():
+            nc.vector.memset(bias_row[:], 0.0)
+            nc.vector.memset(ones[:], 1.0)
+            nc.vector.memset(c_grouped[:], 0.0)
+            make_identity(nc, ident_f32[:])
+            make_identity(nc, ident_bf16[:])
+            nc.sync.dma_start(out=x_sb[:], in_=normalized_resid_pre.rearrange("o t d -> (o t) d"))
+            nc.sync.dma_start(out=bias_row[0:1, :], in_=b_C.rearrange("(o n) k -> o (n k)", o=1))
+            nc.sync.dma_start(out=wc_raw[:], in_=W_C.rearrange("n (p j) k -> p n j k", j=PACK))
+            for step in range(RAW_BUFS):
+                load_wk(step)
 
-        ident_f32 = keep.tile([P, P], F32)
-        make_identity(nc, ident_f32[:])
-        ident_bf16 = keep.tile([P, P], BF16)
-        make_identity(nc, ident_bf16[:])
-        ones = keep.tile([P, P], BF16)
-        nc.vector.memset(ones[:], 1.0)
-        c_grouped = keep.tile([P, 2, 2, TOKENS, PACK], BF16, align_bytes=64)
-        nc.vector.memset(c_grouped[:], 0.0)
-
-        bias_acc = acc_pool.tile([P, JOINT], F32, tag="acc")
-        nc.tensor.matmul(out=bias_acc[:], lhsT=ones[:], rhs=bias_row[:], start=True, stop=True)
-        bias_sb = keep.tile([P, JOINT], F32)
-        nc.scalar.copy(out=bias_sb[:], in_=bias_acc[:])
-
-        x_words = x_sb[:].bitcast(F32).rearrange("t (p j) -> t j p", j=2)
-        x_t = acc_pool.tile([P, 2, TOKENS], F32, tag="acc")
-        for j in range(2):
-            nc.tensor.transpose(x_t[:, j, :], x_words[:, j, :], ident_f32[:])
-        x_grouped = keep.tile([P, TOKENS * PACK], BF16, align_bytes=64)
-        nc.vector.tensor_copy(
-            out=x_grouped[:].bitcast(F32).rearrange("p (t j) -> p t j", j=2),
-            in_=x_t[:].rearrange("p j t -> p t j"),
-        )
-        x_codes = keep.tile([P, TOKENS], U32, align_bytes=64)
-        x_scales = keep.tile([P, TOKENS], U8, align_bytes=64)
-
-        wc_grouped = keep.tile([P, HEADS, D_HEAD, PACK], BF16, align_bytes=64)
-        nc.vector.tensor_copy(out=wc_grouped[:], in_=wc_raw[:].rearrange("p n j k -> p n k j"))
-        wc_codes = keep.tile([P, JOINT], U32, align_bytes=64)
-        wc_scales = keep.tile([P, JOINT], U8, align_bytes=64)
-        nc.vector.quantize_mx(
-            out=x_codes[:].bitcast(FP8X4), scales=x_scales[:], in_=x_grouped[:]
-        )
-        nc.vector.quantize_mx(
-            out=wc_codes[:].bitcast(FP8X4),
-            scales=wc_scales[:],
-            in_=wc_grouped[:].rearrange("p n k j -> p (n k j)"),
-        )
-
-        c_acc = acc_pool.tile([P, JOINT], F32, tag="acc")
-        nc.tensor.matmul_mx(
-            out=c_acc[:],
-            lhsT=x_codes[:].bitcast(FP8X4),
-            lhsT_scale=x_scales[:],
-            rhs=wc_codes[:].bitcast(FP8X4),
-            rhs_scale=wc_scales[:],
-            start=True,
-            stop=True,
-        )
-        c_sorted = keep.tile([P, HEADS, 2, 2, HALF], BF16)
-        for copy in range(2):
-            nc.vector.tensor_tensor(
-                out=c_sorted[:, :, :, copy, :],
-                in0=c_acc[:].rearrange("t (n w e) -> t n e w", n=HEADS, e=2),
-                in1=bias_sb[:].rearrange("t (n w e) -> t n e w", n=HEADS, e=2),
-                op=ADD,
-            )
-        c_t = acc_pool.tile([P, HEADS * 2, TOKENS], BF16, tag="acc")
-        for n in range(HEADS):
-            for e in range(2):
-                nc.tensor.transpose(
-                    c_t[:, 2 * n + e, :],
-                    c_sorted[:, n, e, :, :].rearrange("t c w -> t (c w)"),
-                    ident_bf16[:],
-                )
-        for half in range(2):
-            partitions = slice(half * HALF, (half + 1) * HALF)
+        def quantise_x_and_wc():
+            x_words = x_sb[:].bitcast(F32).rearrange("t (p j) -> t j p", j=2)
+            x_t = acc_pool.tile([P, 2, TOKENS], F32, tag="acc")
+            for j in range(2):
+                nc.tensor.transpose(x_t[:, j, :], x_words[:, j, :], ident_f32[:])
             nc.vector.tensor_copy(
-                out=c_grouped[partitions, half, :, :, :],
-                in_=c_t[partitions, :, :].rearrange("q (u x) t -> q u t x", u=2),
+                out=x_grouped[:].bitcast(F32).rearrange("p (t j) -> p t j", j=2),
+                in_=x_t[:].rearrange("p j t -> p t j"),
             )
-        c_codes = keep.tile([P, 4 * TOKENS], U32, align_bytes=64)
-        c_scales = keep.tile([P, 4 * TOKENS], U8, align_bytes=64)
-        nc.vector.quantize_mx(
-            out=c_codes[:].bitcast(FP8X4),
-            scales=c_scales[:],
-            in_=c_grouped[:].rearrange("q h u t x -> q (h u t x)"),
-        )
+            bias_acc = acc_pool.tile([P, JOINT], F32, tag="acc")
+            nc.tensor.matmul(out=bias_acc[:], lhsT=ones[:], rhs=bias_row[:], start=True, stop=True)
+            nc.scalar.copy(out=bias_sb[:], in_=bias_acc[:])
+            nc.vector.tensor_copy(out=wc_grouped[:], in_=wc_raw[:].rearrange("p n j k -> p n k j"))
+            nc.vector.quantize_mx(
+                out=x_codes[:].bitcast(FP8X4), scales=x_scales[:], in_=x_grouped[:]
+            )
+            nc.vector.quantize_mx(
+                out=wc_codes[:].bitcast(FP8X4),
+                scales=wc_scales[:],
+                in_=wc_grouped[:].rearrange("p n k j -> p (n k j)"),
+            )
 
-        def transpose_wk(raw):
-            words = raw[:].bitcast(F32).rearrange("p (a s w) -> p a s w", a=2, s=WINDOWS)
+        def first_product():
+            c_acc = acc_pool.tile([P, JOINT], F32, tag="acc")
+            nc.tensor.matmul_mx(
+                out=c_acc[:],
+                lhsT=x_codes[:].bitcast(FP8X4),
+                lhsT_scale=x_scales[:],
+                rhs=wc_codes[:].bitcast(FP8X4),
+                rhs_scale=wc_scales[:],
+                start=True,
+                stop=True,
+            )
+            for copy in range(2):
+                nc.vector.tensor_tensor(
+                    out=c_sorted[:, :, :, copy, :],
+                    in0=c_acc[:].rearrange("t (n w e) -> t n e w", n=HEADS, e=2),
+                    in1=bias_sb[:].rearrange("t (n w e) -> t n e w", n=HEADS, e=2),
+                    op=ADD,
+                )
+
+        def quantise_c():
+            c_t = acc_pool.tile([P, HEADS * 2, TOKENS], BF16, tag="acc")
+            for n in range(HEADS):
+                for e in range(2):
+                    nc.tensor.transpose(
+                        c_t[:, 2 * n + e, :],
+                        c_sorted[:, n, e, :, :].rearrange("t c w -> t (c w)"),
+                        ident_bf16[:],
+                    )
+            for half in range(2):
+                partitions = slice(half * HALF, (half + 1) * HALF)
+                nc.vector.tensor_copy(
+                    out=c_grouped[partitions, half, :, :, :],
+                    in_=c_t[partitions, :, :].rearrange("q (u x) t -> q u t x", u=2),
+                )
+            nc.vector.quantize_mx(
+                out=c_codes[:].bitcast(FP8X4),
+                scales=c_scales[:],
+                in_=c_grouped[:].rearrange("q h u t x -> q (h u t x)"),
+            )
+
+        def transpose_wk(step):
+            words = raw_tiles[step][:].bitcast(F32).rearrange(
+                "p (a s w) -> p a s w", a=2, s=WINDOWS
+            )
             grouped = grouped_pool.tile([P, STEP_COLS * PACK], BF16, align_bytes=64)
             grouped_words = grouped[:].bitcast(F32).rearrange("q (s p a) -> q s p a", p=P, a=2)
             for bank in range(STEP_BANKS):
@@ -164,16 +173,23 @@ def tile_trittentioncube_pa_kernel(tc, normalized_resid_pre, W_C, b_C, W_K, out)
                     out=grouped_words[:, first : first + BANK_WINDOWS, :, :],
                     in_=xt[:].rearrange("q s a p -> q s p a"),
                 )
-            return grouped
+            grouped_tiles[step] = grouped
+            if step + RAW_BUFS < STEPS:
+                load_wk(step + RAW_BUFS)
 
-        def quantise_wk(grouped):
+        def quantise_wk(step):
             codes = quantised_pool.tile([P, STEP_COLS], U32, align_bytes=64)
             scales = quantised_pool.tile([P, STEP_COLS], U8, align_bytes=64)
-            nc.vector.quantize_mx(out=codes[:].bitcast(FP8X4), scales=scales[:], in_=grouped[:])
-            return codes, scales
+            nc.vector.quantize_mx(
+                out=codes[:].bitcast(FP8X4), scales=scales[:], in_=grouped_tiles[step][:]
+            )
+            quantised[step] = (codes, scales)
 
-        def multiply(chunk, part, result):
-            sorted_result = result[:].rearrange(
+        def multiply(chunk, part):
+            if part == 0:
+                result = result_pool.tile([P, CHUNK], F32)
+                results[chunk] = result
+            sorted_result = results[chunk][:].rearrange(
                 "t (p b s h) -> t b p s h", b=STEP_BANKS, s=BANK_WINDOWS, h=2
             )
             for bank in (2 * part, 2 * part + 1):
@@ -196,24 +212,24 @@ def tile_trittentioncube_pa_kernel(tc, normalized_resid_pre, W_C, b_C, W_K, out)
                     out=sorted_result[:, bank],
                     in_=acc[:].rearrange("t h (s p) -> t p s h", s=BANK_WINDOWS),
                 )
+            if part == 1:
+                nc.sync.dma_start(
+                    out=out_cols[:, chunk * CHUNK : (chunk + 1) * CHUNK], in_=results[chunk][:]
+                )
 
-        grouped_tiles = {}
-        quantised = {}
-        results = {}
-        for step in range(STEPS + LAG):
+        start_loads_and_constants()
+        quantise_x_and_wc()
+        transpose_wk(0)
+        first_product()
+        transpose_wk(1)
+        quantise_wk(0)
+        quantise_c()
+        transpose_wk(2)
+        quantise_wk(1)
+        for step in range(LAG, STEPS + LAG):
             if step < STEPS:
-                grouped_tiles[step] = transpose_wk(raw_tiles[step])
-                if step + RAW_BUFS < STEPS:
-                    raw_tiles[step + RAW_BUFS] = load_wk(step + RAW_BUFS)
-            if 1 <= step <= STEPS:
-                quantised[step - 1] = quantise_wk(grouped_tiles[step - 1])
-            if step >= LAG:
-                chunk, part = divmod(step - LAG, 2)
-                if part == 0:
-                    result = result_pool.tile([P, CHUNK], F32)
-                    results[chunk] = result
-                multiply(chunk, part, results[chunk])
-                if part == 1:
-                    nc.sync.dma_start(
-                        out=out_cols[:, chunk * CHUNK : (chunk + 1) * CHUNK], in_=results[chunk][:]
-                    )
+                transpose_wk(step)
+            if step <= STEPS:
+                quantise_wk(step - 1)
+            chunk, part = divmod(step - LAG, 2)
+            multiply(chunk, part)

@@ -30,7 +30,6 @@ BANK_WINDOWS = 2
 STEP_BANKS = WINDOWS // BANK_WINDOWS
 GROUP_COLS = BANK_WINDOWS * P
 
-RAW_BUFS = 8
 LAG = 3
 
 FLOPS = 2 * TOKENS * D_MODEL * JOINT + 2 * TOKENS * JOINT * OUT_COLS
@@ -44,10 +43,9 @@ def tile_trittentioncube_pa_kernel(tc, normalized_resid_pre, W_C, b_C, W_K, out)
     with ExitStack() as ctx:
         ctx.enter_context(tc.manual_schedule())
         keep = ctx.enter_context(tc.tile_pool(name="keep", bufs=1))
-        raw_pool = ctx.enter_context(tc.tile_pool(name="raw", bufs=RAW_BUFS))
+        stream_pool = ctx.enter_context(tc.tile_pool(name="stream", bufs=STEPS))
         grouped_pool = ctx.enter_context(tc.tile_pool(name="grouped", bufs=3))
         quantised_pool = ctx.enter_context(tc.tile_pool(name="quantised", bufs=6))
-        result_pool = ctx.enter_context(tc.tile_pool(name="result", bufs=3))
         xt_pool = ctx.enter_context(tc.psum_pool(name="xt", bufs=4))
         acc_pool = ctx.enter_context(tc.psum_pool(name="acc", bufs=4))
 
@@ -75,7 +73,7 @@ def tile_trittentioncube_pa_kernel(tc, normalized_resid_pre, W_C, b_C, W_K, out)
 
         def load_wk(step):
             chunk, pair = divmod(step, 2)
-            raw = raw_pool.tile([P, 2 * ROWS * D_HEAD], BF16)
+            raw = stream_pool.tile([P, 2 * ROWS * D_HEAD], BF16, tag="stream")
             rows = wk_rows[2 * pair : 2 * pair + 2, chunk * CHUNK : (chunk + 1) * CHUNK, :]
             nc.sync.dma_start(
                 out=raw[:].rearrange("p (a x) -> p a x", a=2),
@@ -92,7 +90,7 @@ def tile_trittentioncube_pa_kernel(tc, normalized_resid_pre, W_C, b_C, W_K, out)
             nc.sync.dma_start(out=x_sb[:], in_=normalized_resid_pre.rearrange("o t d -> (o t) d"))
             nc.sync.dma_start(out=bias_row[0:1, :], in_=b_C.rearrange("(o n) k -> o (n k)", o=1))
             nc.sync.dma_start(out=wc_raw[:], in_=W_C.rearrange("n (p j) k -> p n j k", j=PACK))
-            for step in range(RAW_BUFS):
+            for step in range(STEPS):
                 load_wk(step)
 
         def quantise_x_and_wc():
@@ -174,8 +172,6 @@ def tile_trittentioncube_pa_kernel(tc, normalized_resid_pre, W_C, b_C, W_K, out)
                     in_=xt[:].rearrange("q s a p -> q s p a"),
                 )
             grouped_tiles[step] = grouped
-            if step + RAW_BUFS < STEPS:
-                load_wk(step + RAW_BUFS)
 
         def quantise_wk(step):
             codes = quantised_pool.tile([P, STEP_COLS], U32, align_bytes=64)
@@ -187,7 +183,7 @@ def tile_trittentioncube_pa_kernel(tc, normalized_resid_pre, W_C, b_C, W_K, out)
 
         def multiply(chunk, part):
             if part == 0:
-                result = result_pool.tile([P, CHUNK], F32)
+                result = stream_pool.tile([P, CHUNK], F32, tag="stream")
                 results[chunk] = result
             sorted_result = results[chunk][:].rearrange(
                 "t (p b s h) -> t b p s h", b=STEP_BANKS, s=BANK_WINDOWS, h=2

@@ -84,9 +84,9 @@ def tile_trittentioncube_pa_kernel(tc, normalized_resid_pre, W_C, b_C, W_K, out)
         def start_loads_and_constants():
             nc.vector.memset(bias_row[:], 0.0)
             nc.vector.memset(ones[:], 1.0)
-            nc.vector.memset(c_grouped[:], 0.0)
             make_identity(nc, ident_f32[:])
             make_identity(nc, ident_bf16[:])
+            nc.gpsimd.memset(c_grouped[:], 0.0)
             nc.sync.dma_start(out=x_sb[:], in_=normalized_resid_pre.rearrange("o t d -> (o t) d"))
             nc.sync.dma_start(out=bias_row[0:1, :], in_=b_C.rearrange("(o n) k -> o (n k)", o=1))
             nc.sync.dma_start(out=wc_raw[:], in_=W_C.rearrange("n (p j) k -> p n j k", j=PACK))
@@ -215,11 +215,11 @@ def tile_trittentioncube_pa_kernel(tc, normalized_resid_pre, W_C, b_C, W_K, out)
 
         start_loads_and_constants()
         quantise_x_and_wc()
-        transpose_wk(0)
         first_product()
+        transpose_wk(0)
+        quantise_c()
         transpose_wk(1)
         quantise_wk(0)
-        quantise_c()
         transpose_wk(2)
         quantise_wk(1)
         for step in range(LAG, STEPS + LAG):

@@ -204,10 +204,11 @@ def tile_trittentioncube_pa_kernel(tc, normalized_resid_pre, W_C, b_C, W_K, out)
                             start=(pair == 0),
                             stop=(pair == 1),
                         )
-                nc.vector.tensor_copy(
-                    out=sorted_result[:, bank],
-                    in_=acc[:].rearrange("t h (s p) -> t p s h", s=BANK_WINDOWS),
-                )
+                sorted_acc = acc[:].rearrange("t h (s p) -> t p s h", s=BANK_WINDOWS)
+                if bank == STEP_BANKS - 1:
+                    nc.scalar.copy(out=sorted_result[:, bank], in_=sorted_acc)
+                else:
+                    nc.vector.tensor_copy(out=sorted_result[:, bank], in_=sorted_acc)
             if part == 1:
                 nc.sync.dma_start(
                     out=out_cols[:, chunk * CHUNK : (chunk + 1) * CHUNK], in_=results[chunk][:]

@@ -28,9 +28,11 @@ WINDOWS = ROWS // 2
 STEP_COLS = WINDOWS * P
 BANK_WINDOWS = 2
 STEP_BANKS = WINDOWS // BANK_WINDOWS
-GROUP_COLS = BANK_WINDOWS * P
+HALF_COLS = STEP_COLS // 2
+GROUP_COLS = 256
+GROUP_WINDOWS = GROUP_COLS // HALF
 
-LAG = 3
+BANK_LAG = 6
 
 FLOPS = 2 * TOKENS * D_MODEL * JOINT + 2 * TOKENS * JOINT * OUT_COLS
 
@@ -160,7 +162,9 @@ def tile_trittentioncube_pa_kernel(tc, normalized_resid_pre, W_C, b_C, W_K, out)
                 "p (a s w) -> p a s w", a=2, s=WINDOWS
             )
             grouped = grouped_pool.tile([P, STEP_COLS * PACK], BF16, align_bytes=64)
-            grouped_words = grouped[:].bitcast(F32).rearrange("q (s p a) -> q s p a", p=P, a=2)
+            grouped_words = grouped[:].bitcast(F32).rearrange(
+                "q (f s p a) -> q s f p a", f=2, s=WINDOWS, a=2
+            )
             for bank in range(STEP_BANKS):
                 first = bank * BANK_WINDOWS
                 xt = xt_pool.tile([P, BANK_WINDOWS, 2, P], F32)
@@ -168,51 +172,62 @@ def tile_trittentioncube_pa_kernel(tc, normalized_resid_pre, W_C, b_C, W_K, out)
                     for a in range(2):
                         nc.tensor.transpose(xt[:, s, a, :], words[:, a, first + s, :], ident_f32[:])
                 nc.scalar.copy(
-                    out=grouped_words[:, first : first + BANK_WINDOWS, :, :],
-                    in_=xt[:].rearrange("q s a p -> q s p a"),
+                    out=grouped_words[:, first : first + BANK_WINDOWS],
+                    in_=xt[:].rearrange("q s a (f p) -> q s f p a", f=2),
                 )
             grouped_tiles[step] = grouped
 
-        def quantise_wk(step):
-            codes = quantised_pool.tile([P, STEP_COLS], U32, align_bytes=64)
-            scales = quantised_pool.tile([P, STEP_COLS], U8, align_bytes=64)
+        def quantise_wk(step, first, last):
+            if first == 0:
+                codes = quantised_pool.tile([P, STEP_COLS], U32, align_bytes=64)
+                scales = quantised_pool.tile([P, STEP_COLS], U8, align_bytes=64)
+                quantised[step] = (codes, scales)
+            codes, scales = quantised[step]
             nc.vector.quantize_mx(
-                out=codes[:].bitcast(FP8X4), scales=scales[:], in_=grouped_tiles[step][:]
+                out=codes[:, first:last].bitcast(FP8X4),
+                scales=scales[:, first:last],
+                in_=grouped_tiles[step][:, first * PACK : last * PACK],
             )
-            quantised[step] = (codes, scales)
 
-        def multiply(chunk, part):
-            if part == 0:
+        def store(chunk, first, last):
+            nc.sync.dma_start(
+                out=out_cols[:, chunk * CHUNK + first : chunk * CHUNK + last],
+                in_=results[chunk][:, first:last],
+            )
+
+        def multiply(index):
+            chunk, part, bank = index // 4, index // 2 % 2, index % 2
+            if part == bank == 0:
                 result = stream_pool.tile([P, CHUNK], F32, tag="stream")
                 results[chunk] = result
             sorted_result = results[chunk][:].rearrange(
-                "t (p b s h) -> t b p s h", b=STEP_BANKS, s=BANK_WINDOWS, h=2
+                "t (f p b s h) -> t f b p s h", f=2, b=2, s=GROUP_WINDOWS, h=2
             )
-            for bank in (2 * part, 2 * part + 1):
-                cols = slice(bank * GROUP_COLS, (bank + 1) * GROUP_COLS)
-                acc = acc_pool.tile([P, 2, GROUP_COLS], F32, tag="acc")
-                for half in range(2):
-                    for pair in range(2):
-                        codes, scales = quantised[2 * chunk + pair]
-                        tokens = slice((2 * half + pair) * TOKENS, (2 * half + pair + 1) * TOKENS)
-                        nc.tensor.matmul_mx(
-                            out=acc[:, half, :],
-                            lhsT=c_codes[:, tokens].bitcast(FP8X4),
-                            lhsT_scale=c_scales[:, tokens],
-                            rhs=codes[:, cols].bitcast(FP8X4),
-                            rhs_scale=scales[:, cols],
-                            start=(pair == 0),
-                            stop=(pair == 1),
-                        )
-                sorted_acc = acc[:].rearrange("t h (s p) -> t p s h", s=BANK_WINDOWS)
-                if bank == STEP_BANKS - 1:
-                    nc.scalar.copy(out=sorted_result[:, bank], in_=sorted_acc)
-                else:
-                    nc.vector.tensor_copy(out=sorted_result[:, bank], in_=sorted_acc)
-            if part == 1:
-                nc.sync.dma_start(
-                    out=out_cols[:, chunk * CHUNK : (chunk + 1) * CHUNK], in_=results[chunk][:]
-                )
+            first = part * HALF_COLS + bank * GROUP_COLS
+            cols = slice(first, first + GROUP_COLS)
+            acc = acc_pool.tile([P, 2, GROUP_COLS], F32, tag="acc")
+            for half in range(2):
+                for pair in range(2):
+                    codes, scales = quantised[2 * chunk + pair]
+                    tokens = slice((2 * half + pair) * TOKENS, (2 * half + pair + 1) * TOKENS)
+                    nc.tensor.matmul_mx(
+                        out=acc[:, half, :],
+                        lhsT=c_codes[:, tokens].bitcast(FP8X4),
+                        lhsT_scale=c_scales[:, tokens],
+                        rhs=codes[:, cols].bitcast(FP8X4),
+                        rhs_scale=scales[:, cols],
+                        start=(pair == 0),
+                        stop=(pair == 1),
+                    )
+            sorted_acc = acc[:].rearrange("t h (s p) -> t p s h", s=GROUP_WINDOWS)
+            if part == bank == 1:
+                nc.scalar.copy(out=sorted_result[:, part, bank], in_=sorted_acc)
+            else:
+                nc.vector.tensor_copy(out=sorted_result[:, part, bank], in_=sorted_acc)
+            if bank == 1 and chunk == CHUNKS - 1:
+                store(chunk, part * CHUNK // 2, (part + 1) * CHUNK // 2)
+            elif bank == 1 and part == 1:
+                store(chunk, 0, CHUNK)
 
         start_loads_and_constants()
         quantise_x_and_wc()
@@ -220,13 +235,14 @@ def tile_trittentioncube_pa_kernel(tc, normalized_resid_pre, W_C, b_C, W_K, out)
         transpose_wk(0)
         quantise_c()
         transpose_wk(1)
-        quantise_wk(0)
-        transpose_wk(2)
-        quantise_wk(1)
-        for step in range(LAG, STEPS + LAG):
-            if step < STEPS:
-                transpose_wk(step)
-            if step <= STEPS:
-                quantise_wk(step - 1)
-            chunk, part = divmod(step - LAG, 2)
-            multiply(chunk, part)
+        quantise_wk(0, 0, STEP_COLS)
+        for step in range(2, STEPS):
+            transpose_wk(step)
+            quantise_wk(step - 1, 0, STEP_COLS)
+            for index in range(max(0, 2 * step - BANK_LAG), 2 * step - BANK_LAG + 2):
+                multiply(index)
+        quantise_wk(STEPS - 1, 0, HALF_COLS)
+        multiply(2 * STEPS - BANK_LAG)
+        quantise_wk(STEPS - 1, HALF_COLS, STEP_COLS)
+        for index in range(2 * STEPS - BANK_LAG + 1, 2 * STEPS):
+            multiply(index)

@@ -90,8 +90,8 @@ def tile_trittentioncube_pa_kernel(tc, normalized_resid_pre, W_C, b_C, W_K, out)
             make_identity(nc, ident_bf16[:])
             nc.gpsimd.memset(c_grouped[:], 0.0)
             nc.sync.dma_start(out=x_sb[:], in_=normalized_resid_pre.rearrange("o t d -> (o t) d"))
-            nc.sync.dma_start(out=bias_row[0:1, :], in_=b_C.rearrange("(o n) k -> o (n k)", o=1))
             nc.sync.dma_start(out=wc_raw[:], in_=W_C.rearrange("n (p j) k -> p n j k", j=PACK))
+            nc.sync.dma_start(out=bias_row[0:1, :], in_=b_C.rearrange("(o n) k -> o (n k)", o=1))
             for step in range(STEPS):
                 load_wk(step)
 

from contextlib import ExitStack

import concourse.mybir as mybir
from concourse.masks import make_identity

F32 = mybir.dt.float32
BF16 = mybir.dt.bfloat16
U32 = mybir.dt.uint32
U8 = mybir.dt.uint8
FP8X4 = mybir.dt.float8_e4m3fn_x4
ADD = mybir.AluOpType.add

P = 128
PACK = 4
TOKENS = 128
D_MODEL = 512
HEADS = 4
D_HEAD = 128
JOINT = HEADS * D_HEAD
OUT_COLS = D_HEAD * D_HEAD
HALF = 64

ROWS = 16
CHUNK = P * ROWS
CHUNKS = OUT_COLS // CHUNK
STEPS = 2 * CHUNKS
WINDOWS = ROWS // 2
STEP_COLS = WINDOWS * P
BANK_WINDOWS = 2
STEP_BANKS = WINDOWS // BANK_WINDOWS
HALF_COLS = STEP_COLS // 2
GROUP_COLS = 256
GROUP_WINDOWS = GROUP_COLS // HALF

BANK_LAG = 6

FLOPS = 2 * TOKENS * D_MODEL * JOINT + 2 * TOKENS * JOINT * OUT_COLS


def tile_trittentioncube_pa_kernel(tc, normalized_resid_pre, W_C, b_C, W_K, out):
    nc = tc.nc
    wk_rows = W_K.rearrange("n i j k -> n (i j) k")
    out_cols = out.rearrange("o t i j -> (o t) (i j)")

    with ExitStack() as ctx:
        ctx.enter_context(tc.manual_schedule())
        keep = ctx.enter_context(tc.tile_pool(name="keep", bufs=1))
        stream_pool = ctx.enter_context(tc.tile_pool(name="stream", bufs=STEPS))
        grouped_pool = ctx.enter_context(tc.tile_pool(name="grouped", bufs=3))
        quantised_pool = ctx.enter_context(tc.tile_pool(name="quantised", bufs=6))
        xt_pool = ctx.enter_context(tc.psum_pool(name="xt", bufs=4))
        acc_pool = ctx.enter_context(tc.psum_pool(name="acc", bufs=4))

        x_sb = keep.tile([P, D_MODEL], BF16)
        wc_raw = keep.tile([P, HEADS, PACK, D_HEAD], BF16)
        bias_row = keep.tile([P, JOINT], BF16)
        bias_sb = keep.tile([P, JOINT], F32)
        ident_f32 = keep.tile([P, P], F32)
        ident_bf16 = keep.tile([P, P], BF16)
        ones = keep.tile([P, P], BF16)
        x_grouped = keep.tile([P, TOKENS * PACK], BF16, align_bytes=64)
        x_codes = keep.tile([P, TOKENS], U32, align_bytes=64)
        x_scales = keep.tile([P, TOKENS], U8, align_bytes=64)
        wc_grouped = keep.tile([P, HEADS, D_HEAD, PACK], BF16, align_bytes=64)
        wc_codes = keep.tile([P, JOINT], U32, align_bytes=64)
        wc_scales = keep.tile([P, JOINT], U8, align_bytes=64)
        c_sorted = keep.tile([P, HEADS, 2, 2, HALF], BF16)
        c_grouped = keep.tile([P, 2, 2, TOKENS, PACK], BF16, align_bytes=64)
        c_codes = keep.tile([P, 4 * TOKENS], U32, align_bytes=64)
        c_scales = keep.tile([P, 4 * TOKENS], U8, align_bytes=64)
        raw_tiles = {}
        grouped_tiles = {}
        quantised = {}
        results = {}

        def load_wk(step):
            chunk, pair = divmod(step, 2)
            raw = stream_pool.tile([P, 2 * ROWS * D_HEAD], BF16, tag="stream")
            rows = wk_rows[2 * pair : 2 * pair + 2, chunk * CHUNK : (chunk + 1) * CHUNK, :]
            nc.sync.dma_start(
                out=raw[:].rearrange("p (a x) -> p a x", a=2),
                in_=rows.rearrange("a (p r) k -> p a (r k)", p=P),
            )
            raw_tiles[step] = raw

        def start_loads_and_constants():
            nc.vector.memset(bias_row[:], 0.0)
            nc.vector.memset(ones[:], 1.0)
            make_identity(nc, ident_f32[:])
            make_identity(nc, ident_bf16[:])
            nc.gpsimd.memset(c_grouped[:], 0.0)
            nc.sync.dma_start(out=x_sb[:], in_=normalized_resid_pre.rearrange("o t d -> (o t) d"))
            nc.sync.dma_start(out=wc_raw[:], in_=W_C.rearrange("n (p j) k -> p n j k", j=PACK))
            nc.sync.dma_start(out=bias_row[0:1, :], in_=b_C.rearrange("(o n) k -> o (n k)", o=1))
            for step in range(STEPS):
                load_wk(step)

        def quantise_x_and_wc():
            x_words = x_sb[:].bitcast(F32).rearrange("t (p j) -> t j p", j=2)
            x_t = acc_pool.tile([P, 2, TOKENS], F32, tag="acc")
            for j in range(2):
                nc.tensor.transpose(x_t[:, j, :], x_words[:, j, :], ident_f32[:])
            nc.vector.tensor_copy(
                out=x_grouped[:].bitcast(F32).rearrange("p (t j) -> p t j", j=2),
                in_=x_t[:].rearrange("p j t -> p t j"),
            )
            bias_acc = acc_pool.tile([P, JOINT], F32, tag="acc")
            nc.tensor.matmul(out=bias_acc[:], lhsT=ones[:], rhs=bias_row[:], start=True, stop=True)
            nc.scalar.copy(out=bias_sb[:], in_=bias_acc[:])
            nc.vector.tensor_copy(out=wc_grouped[:], in_=wc_raw[:].rearrange("p n j k -> p n k j"))
            nc.vector.quantize_mx(
                out=x_codes[:].bitcast(FP8X4), scales=x_scales[:], in_=x_grouped[:]
            )
            nc.vector.quantize_mx(
                out=wc_codes[:].bitcast(FP8X4),
                scales=wc_scales[:],
                in_=wc_grouped[:].rearrange("p n k j -> p (n k j)"),
            )

        def first_product():
            c_acc = acc_pool.tile([P, JOINT], F32, tag="acc")
            nc.tensor.matmul_mx(
                out=c_acc[:],
                lhsT=x_codes[:].bitcast(FP8X4),
                lhsT_scale=x_scales[:],
                rhs=wc_codes[:].bitcast(FP8X4),
                rhs_scale=wc_scales[:],
                start=True,
                stop=True,
            )
            for copy in range(2):
                nc.vector.tensor_tensor(
                    out=c_sorted[:, :, :, copy, :],
                    in0=c_acc[:].rearrange("t (n w e) -> t n e w", n=HEADS, e=2),
                    in1=bias_sb[:].rearrange("t (n w e) -> t n e w", n=HEADS, e=2),
                    op=ADD,
                )

        def quantise_c():
            c_t = acc_pool.tile([P, HEADS * 2, TOKENS], BF16, tag="acc")
            for n in range(HEADS):
                for e in range(2):
                    nc.tensor.transpose(
                        c_t[:, 2 * n + e, :],
                        c_sorted[:, n, e, :, :].rearrange("t c w -> t (c w)"),
                        ident_bf16[:],
                    )
            for half in range(2):
                partitions = slice(half * HALF, (half + 1) * HALF)
                nc.vector.tensor_copy(
                    out=c_grouped[partitions, half, :, :, :],
                    in_=c_t[partitions, :, :].rearrange("q (u x) t -> q u t x", u=2),
                )
            nc.vector.quantize_mx(
                out=c_codes[:].bitcast(FP8X4),
                scales=c_scales[:],
                in_=c_grouped[:].rearrange("q h u t x -> q (h u t x)"),
            )

        def transpose_wk(step):
            words = raw_tiles[step][:].bitcast(F32).rearrange(
                "p (a s w) -> p a s w", a=2, s=WINDOWS
            )
            grouped = grouped_pool.tile([P, STEP_COLS * PACK], BF16, align_bytes=64)
            grouped_words = grouped[:].bitcast(F32).rearrange(
                "q (f s p a) -> q s f p a", f=2, s=WINDOWS, a=2
            )
            for bank in range(STEP_BANKS):
                first = bank * BANK_WINDOWS
                xt = xt_pool.tile([P, BANK_WINDOWS, 2, P], F32)
                for s in range(BANK_WINDOWS):
                    for a in range(2):
                        nc.tensor.transpose(xt[:, s, a, :], words[:, a, first + s, :], ident_f32[:])
                nc.scalar.copy(
                    out=grouped_words[:, first : first + BANK_WINDOWS],
                    in_=xt[:].rearrange("q s a (f p) -> q s f p a", f=2),
                )
            grouped_tiles[step] = grouped

        def quantise_wk(step, first, last):
            if first == 0:
                codes = quantised_pool.tile([P, STEP_COLS], U32, align_bytes=64)
                scales = quantised_pool.tile([P, STEP_COLS], U8, align_bytes=64)
                quantised[step] = (codes, scales)
            codes, scales = quantised[step]
            nc.vector.quantize_mx(
                out=codes[:, first:last].bitcast(FP8X4),
                scales=scales[:, first:last],
                in_=grouped_tiles[step][:, first * PACK : last * PACK],
            )

        def store(chunk, first, last):
            nc.sync.dma_start(
                out=out_cols[:, chunk * CHUNK + first : chunk * CHUNK + last],
                in_=results[chunk][:, first:last],
            )

        def multiply(index):
            chunk, part, bank = index // 4, index // 2 % 2, index % 2
            if part == bank == 0:
                result = stream_pool.tile([P, CHUNK], F32, tag="stream")
                results[chunk] = result
            sorted_result = results[chunk][:].rearrange(
                "t (f p b s h) -> t f b p s h", f=2, b=2, s=GROUP_WINDOWS, h=2
            )
            first = part * HALF_COLS + bank * GROUP_COLS
            cols = slice(first, first + GROUP_COLS)
            acc = acc_pool.tile([P, 2, GROUP_COLS], F32, tag="acc")
            for half in range(2):
                for pair in range(2):
                    codes, scales = quantised[2 * chunk + pair]
                    tokens = slice((2 * half + pair) * TOKENS, (2 * half + pair + 1) * TOKENS)
                    nc.tensor.matmul_mx(
                        out=acc[:, half, :],
                        lhsT=c_codes[:, tokens].bitcast(FP8X4),
                        lhsT_scale=c_scales[:, tokens],
                        rhs=codes[:, cols].bitcast(FP8X4),
                        rhs_scale=scales[:, cols],
                        start=(pair == 0),
                        stop=(pair == 1),
                    )
            sorted_acc = acc[:].rearrange("t h (s p) -> t p s h", s=GROUP_WINDOWS)
            if part == bank == 1:
                nc.scalar.copy(out=sorted_result[:, part, bank], in_=sorted_acc)
            else:
                nc.vector.tensor_copy(out=sorted_result[:, part, bank], in_=sorted_acc)
            if bank == 1 and chunk == CHUNKS - 1:
                store(chunk, part * CHUNK // 2, (part + 1) * CHUNK // 2)
            elif bank == 1 and part == 1:
                store(chunk, 0, CHUNK)

        start_loads_and_constants()
        quantise_x_and_wc()
        first_product()
        transpose_wk(0)
        quantise_c()
        transpose_wk(1)
        quantise_wk(0, 0, STEP_COLS)
        for step in range(2, STEPS):
            transpose_wk(step)
            quantise_wk(step - 1, 0, STEP_COLS)
            for index in range(max(0, 2 * step - BANK_LAG), 2 * step - BANK_LAG + 2):
                multiply(index)
        quantise_wk(STEPS - 1, 0, HALF_COLS)
        multiply(2 * STEPS - BANK_LAG)
        quantise_wk(STEPS - 1, HALF_COLS, STEP_COLS)
        for index in range(2 * STEPS - BANK_LAG + 1, 2 * STEPS):
            multiply(index)
